import numpy as np
import ml_dtypes


def mxq(x, axis, fmt="e4m3"):
    dtype, down = {"e4m3": (ml_dtypes.float8_e4m3fn, 7), "e5m2": (ml_dtypes.float8_e5m2, 14)}[fmt]
    v = np.moveaxis(np.asarray(x, np.float32).astype(ml_dtypes.bfloat16).astype(np.float64), axis, -1)
    blocks = v.reshape(v.shape[:-1] + (-1, 32))
    amax = np.abs(blocks).max(-1, keepdims=True)
    byte = np.maximum(np.where(amax > 0, np.frexp(amax)[1] - 1 + 127, 0) - down, 1)
    scale = np.exp2(byte - 127.0)
    codes = (blocks / scale).astype(np.float32).astype(dtype).astype(np.float64)
    return np.moveaxis((codes * scale).reshape(v.shape), -1, axis)


WIDE = False


def mx_kscale(k):
    if not WIDE:
        return np.ones(k)
    levels = np.array([10, -10, 5, -5, 0])
    if k % 512:
        return np.exp2(np.random.permutation(np.resize(levels, k // 32))).repeat(32)
    a = np.empty((k // 512, 16))
    for p in range(k // 512):
        a[p, :8] = np.random.permutation(np.resize(levels, 8))
        for g in range(8):
            far = levels[np.abs(levels - a[p, g]) >= 10]
            a[p, g + 8] = far[np.random.randint(len(far))]
    return np.exp2(a.ravel()).repeat(32)


BF16 = ml_dtypes.bfloat16


def bf(x):
    return np.asarray(x, np.float32).astype(BF16)


def f64(x):
    return np.asarray(x).astype(np.float64)


B, DIM, E, HID = 1024, 1024, 1024, 2048
EPS = 1e-5


def layer_norm(y, g, b):
    m = y.mean(-1, keepdims=True)
    v = ((y - m) ** 2).mean(-1, keepdims=True)
    return (y - m) / np.sqrt(v + EPS) * g + b


def draw0():
    s, t = mx_kscale(DIM), mx_kscale(E)
    r = np.random.standard_normal
    return {'feat': bf(r((B, DIM))),
            'own_self': bf(r((B, DIM))),
            'other_self': bf(r((B, DIM)) * s),
            'Wv': bf(r((E, DIM)) / np.sqrt(DIM) / s[None, :] * t[:, None]),
            'bv': bf(r(E) * 0.2 * t),
            'Wo': bf(r((DIM, E)) / np.sqrt(E) / t[None, :]),
            'bo': bf(r(DIM) * 0.2),
            'g': bf(1.0 + 0.1 * r(DIM)),
            'be': bf(0.1 * r(DIM))}


def core(feat, own_self, other_self, Wv, bv, Wo, bo, g, be):
    val = (mxq(f64(other_self), 1, 'e4m3') @ mxq(f64(Wv), 1, 'e4m3').T) + f64(bv)
    cross = (mxq(val, 1, 'e4m3') @ mxq(f64(Wo), 1, 'e4m3').T) + f64(bo)
    return layer_norm(f64(feat) + (f64(own_self) + cross) * 0.5, f64(g), f64(be))


def e4m3fn_bytes(y):
    return np.clip(np.asarray(y, np.float64), -448.0, 448.0).astype(np.float32).astype(ml_dtypes.float8_e4m3fn).view(np.uint8)


def e4m3fn_values(b):
    return np.asarray(b, np.uint8).view(ml_dtypes.float8_e4m3fn).astype(np.float64)


def setup_inputs():
    d = draw0()
    x0 = np.asarray(d['other_self']).astype(np.float64)
    s = (np.max(np.abs(x0), axis=(0,), keepdims=True) / 448.0).astype(np.float32)
    out = {}
    for k, v in d.items():
        if k == 'other_self':
            out['other_self_bytes'] = e4m3fn_bytes(x0 / s.astype(np.float64))
            out['other_self_scale'] = s
        else:
            out[k] = v
    return out


def reference(feat, own_self, other_self_bytes, other_self_scale, Wv, bv, Wo, bo, g, be):
    return core(feat, own_self, e4m3fn_values(other_self_bytes) * other_self_scale.astype(np.float64), Wv, bv, Wo, bo, g, be)

@@ -1,0 +1,379 @@
+from contextlib import ExitStack
+
+import concourse.mybir as mybir
+from concourse.masks import make_identity
+
+FLOPS = 2 * 2 * 1024 * 1024 * 1024
+
+F32 = mybir.dt.float32
+BF16 = mybir.dt.bfloat16
+U32 = mybir.dt.uint32
+U8 = mybir.dt.uint8
+E4M3 = mybir.dt.float8_e4m3fn
+X4 = mybir.dt.float8_e4m3fn_x4
+ACT = mybir.ActivationFunctionType
+ALU = mybir.AluOpType
+
+P = 128
+D = 1024
+NB = 8
+EPS = 1e-5
+OWN_ON_T = ()
+
+
+def tile_efficientfusionlayer_pb_kernel(
+    tc, feat, own_self, xbytes, xscale, Wv, bv, Wo, bo, g, be, out
+):
+    nc = tc.nc
+    with ExitStack() as ctx:
+        const = ctx.enter_context(tc.tile_pool(name="const", bufs=1))
+        ring = ctx.enter_context(tc.tile_pool(name="ring", bufs=1))
+        work = ctx.enter_context(tc.tile_pool(name="work", bufs=2))
+        psum = ctx.enter_context(tc.psum_pool(name="psum", bufs=8))
+
+        ctx.enter_context(tc.manual_schedule())
+        sc = const.tile([P, D], F32, name="sc")
+        nc.scalar.dma_start(out=sc[:], in_=xscale.rearrange("o k -> (o k)").partition_broadcast(P))
+        wv_raw = [[ring.tile([P, 2, D], BF16, name=f"wv{gg}{tp}", tag="wraw", bufs=8) for tp in range(2)] for gg in range(2)]
+        wvsrc = Wv.rearrange("(g m t) k -> g m t k", g=2, t=4)
+        xb = [const.tile([P, 2, D], U8, name=f"xb{c}") for c in range(4)]
+        xsrc = xbytes.rearrange("(c i p) k -> c p i k", c=4, i=2)
+
+        def load_wv(gg, tp):
+            nc.sync.dma_start(out=wv_raw[gg][tp][:], in_=wvsrc[gg, :, 2 * tp : 2 * tp + 2, :])
+
+        def load_x(c):
+            nc.sync.dma_start(out=xb[c][:], in_=xsrc[c])
+
+        load_wv(0, 0)
+        load_x(0)
+        load_wv(0, 1)
+        load_x(1)
+        load_wv(1, 0)
+        load_wv(1, 1)
+        load_x(2)
+        load_x(3)
+        bv_t = const.tile([P, 2, 4], BF16, name="bv_t")
+        nc.scalar.dma_start(out=bv_t[:], in_=bv.rearrange("(g p t) -> p g t", g=2, t=4))
+        bo_rows = const.tile([P, P], BF16, name="bo_rows")
+        nc.gpsimd.memset(bo_rows[:], 0.0)
+        nc.scalar.dma_start(out=bo_rows[0:8, :], in_=bo.rearrange("(j p) -> j p", p=P))
+        wo_raw = [ring.tile([P, 2, D], BF16, name=f"wo{jp}", tag="wraw", bufs=8) for jp in range(4)]
+        wosrc = Wo.rearrange("(q j m) e -> q m j e", q=4, j=2)
+        for jp in range(4):
+            nc.sync.dma_start(out=wo_raw[jp][:], in_=wosrc[jp])
+        g_b = const.tile([P, D], BF16, name="g_b")
+        be_b = const.tile([P, D], BF16, name="be_b")
+        ft = [const.tile([P, D], BF16, name=f"ft{i}") for i in range(NB)]
+        ow = [const.tile([P, D], BF16, name=f"ow{i}") for i in range(NB)]
+        for i in range(NB):
+            nc.sync.dma_start(out=ft[i][:], in_=feat[P * i : P * (i + 1), :])
+            nc.sync.dma_start(out=ow[i][:], in_=own_self[P * i : P * (i + 1), :])
+            if i == 1:
+                nc.sync.dma_start(out=g_b[:], in_=g.partition_broadcast(P))
+                nc.sync.dma_start(out=be_b[:], in_=be.partition_broadcast(P))
+
+        id32 = const.tile([P, P], F32, name="id32")
+        make_identity(nc, id32[:])
+        id16 = const.tile([P, P], BF16, name="id16")
+        nc.vector.tensor_copy(out=id16[:], in_=id32[:])
+        ih16 = const.tile([P, P], BF16, name="ih16")
+        nc.vector.tensor_scalar(out=ih16[:], in0=id32[:], scalar1=0.5, scalar2=None, op0=ALU.mult)
+
+        xs = {}
+        xg = {}
+        wvg = {}
+        wog = {}
+        ct = {}
+
+        def grp(name):
+            return ring.tile([P, 2, 256, 2], F32, name=name, tag="grp", bufs=8, align_bytes=64)
+
+        xc = const.tile([P, 2, D], U32, name="xc", align_bytes=64)
+        xsca = const.tile([P, 2, D], U8, name="xsca", align_bytes=64)
+        wvc = const.tile([P, 2, D], U32, name="wvc", align_bytes=64)
+        wvs = const.tile([P, 2, D], U8, name="wvs", align_bytes=64)
+        woc = const.tile([P, 2, D], U32, name="woc", align_bytes=64)
+        wos = const.tile([P, 2, D], U8, name="wos", align_bytes=64)
+        vg = {}
+        vc = const.tile([P, 2, D], U32, name="vc", align_bytes=64)
+        vs = const.tile([P, 2, D], U8, name="vs", align_bytes=64)
+        boh = const.tile([P, 8], F32, name="boh")
+
+        def turn(rows, dst):
+            words = rows.bitcast(F32)
+            bank = psum.tile([P, 2, 2, P], F32, name="tp", tag="ps")
+            for h in range(2):
+                for u in range(2):
+                    nc.tensor.transpose(bank[:, h, u, :], words[:, 256 * h + u : 256 * (h + 1) : 2], id32[:])
+            nc.scalar.copy(out=dst, in_=bank[:].rearrange("p h u r -> p h r u"))
+
+        def quant(codes, scales, grouped, cols):
+            for h in range(2):
+                nc.vector.quantize_mx(
+                    out=codes[:, h, cols].bitcast(X4),
+                    scales=scales[:, h, cols],
+                    in_=grouped[:, h].rearrange("p r u -> p (r u)").bitcast(BF16),
+                )
+
+        def scale_x(i):
+            xs[i] = ring.tile([P, D], BF16, name=f"xs{i}", tag="xs", bufs=4)
+            nc.vector.tensor_tensor(
+                out=xs[i][:], in0=xb[i // 2][:, i % 2, :].bitcast(E4M3), in1=sc[:], op=ALU.mult
+            )
+
+        def turn_x(i):
+            if i % 2 == 0:
+                xg[i // 2] = grp(f"xg{i}")
+            turn(xs[i][:], xg[i // 2][:, :, P * (i % 2) : P * (i % 2 + 1), :])
+
+        def turn_wv(gg, t):
+            if t % 2 == 0:
+                wvg[gg, t // 2] = grp(f"wvg{gg}{t}")
+            turn(wv_raw[gg][t // 2][:, t % 2, :], wvg[gg, t // 2][:, :, P * (t % 2) : P * (t % 2 + 1), :])
+
+        def turn_wo(j):
+            if j % 2 == 0:
+                wog[j // 2] = grp(f"wog{j}")
+            turn(wo_raw[j // 2][:, j % 2, :], wog[j // 2][:, :, P * (j % 2) : P * (j % 2 + 1), :])
+
+        s1 = {}
+
+        def stage1(i, gg):
+            bank = psum.tile([P, 4, P], F32, name="s1", tag="ps")
+            s1[i, gg] = bank
+            for t in range(4):
+                lc = slice(512 * gg + P * t, 512 * gg + P * (t + 1))
+                rc = slice(P * i, P * (i + 1))
+                for h in range(2):
+                    nc.tensor.matmul_mx(
+                        out=bank[:, t, :],
+                        lhsT=wvc[:, h, lc].bitcast(X4),
+                        lhsT_scale=wvs[:, h, lc],
+                        rhs=xc[:, h, rc].bitcast(X4),
+                        rhs_scale=xsca[:, h, rc],
+                        start=(h == 0),
+                        stop=(h == 1),
+                    )
+
+        def bias_v(i, gg):
+            if i % 2 == 0:
+                vg[i // 2, gg] = ring.tile([P, 256, 4], BF16, name=f"vg{i}{gg}", tag="vg", bufs=5, align_bytes=64)
+            nc.vector.tensor_tensor(
+                out=vg[i // 2, gg][:, P * (i % 2) : P * (i % 2 + 1), :],
+                in0=s1[i, gg][:].rearrange("p t b -> p b t"),
+                in1=bv_t[:, gg, :].unsqueeze(1).to_broadcast([P, P, 4]),
+                op=ALU.add,
+            )
+
+        def quant_v(q):
+            for gg in range(2):
+                cols = slice(256 * q, 256 * (q + 1))
+                nc.vector.quantize_mx(
+                    out=vc[:, gg, cols].bitcast(X4),
+                    scales=vs[:, gg, cols],
+                    in_=vg[q, gg][:].rearrange("p b t -> p (b t)"),
+                )
+
+        def stage2(c, j):
+            bank = psum.tile([P, 512], F32, name="s2", tag="ps")
+            ct[c, j] = ring.tile([P, 512], F32, name=f"ct{c}{j}", tag="ct", bufs=16)
+            lc = slice(P * j, P * (j + 1))
+            rc = slice(512 * c, 512 * (c + 1))
+            for gg in range(2):
+                nc.tensor.matmul_mx(
+                    out=bank[:],
+                    lhsT=woc[:, gg, lc].bitcast(X4),
+                    lhsT_scale=wos[:, gg, lc],
+                    rhs=vc[:, gg, rc].bitcast(X4),
+                    rhs_scale=vs[:, gg, rc],
+                    start=(gg == 0),
+                    stop=(gg == 1),
+                )
+            nc.scalar.activation(out=ct[c, j][:], in_=bank[:], func=ACT.Identity, bias=boh[:, j : j + 1], scale=0.5)
+
+        zb, zs_, qt, rs, nmean = {}, {}, {}, {}, {}
+
+        def zsum(i):
+            c, sl = i // 4, slice(P * (i % 4), P * (i % 4 + 1))
+            for hd in range(2):
+                z = psum.tile([P, 512], F32, name="z", tag="ps")
+                cols = slice(512 * hd, 512 * (hd + 1))
+                nc.tensor.matmul(out=z[:], lhsT=id16[:], rhs=ft[i][:, cols], start=True, stop=False)
+                if i in OWN_ON_T:
+                    nc.tensor.matmul(out=z[:], lhsT=ih16[:], rhs=ow[i][:, cols], start=False, stop=False)
+                zb[i, hd] = z
+            for hd in range(2):
+                for jj in range(4):
+                    nc.tensor.matmul(
+                        out=zb[i, hd][:, P * jj : P * (jj + 1)],
+                        lhsT=ct[c, 4 * hd + jj][:, sl],
+                        rhs=id32[:],
+                        start=False,
+                        stop=(jj == 3),
+                        is_transpose=True,
+                    )
+
+        def stats(i):
+            rs[i] = work.tile([P, 1], F32, name="rstd")
+            if i in OWN_ON_T:
+                st = work.tile([P, 2, 6], F32, name="st")
+                mv = work.tile([P, 2], F32, name="mv")
+                for hd in range(2):
+                    nc.vector.bn_stats(out=st[:, hd, :], in_=zb[i, hd][:])
+                nc.vector.bn_aggr(out=mv[:], in_=st[:].rearrange("p a b -> p (a b)"))
+                nc.scalar.activation(out=rs[i][:], in_=mv[:, 1:2], func=ACT.Abs_reciprocal_sqrt, bias=EPS)
+                nmean[i] = mv
+            else:
+                zs = work.tile([P, D], F32, name="zs")
+                sm0 = work.tile([P, 1], F32, name="sm0")
+                sm1 = work.tile([P, 1], F32, name="sm1")
+                nm = work.tile([P, 1], F32, name="nm")
+                sq = work.tile([P, 1], F32, name="sq")
+                junk = work.tile([P, D], BF16, name="junk", bufs=1)
+                for hd, sm in ((0, sm0), (1, sm1)):
+                    cols = slice(512 * hd, 512 * (hd + 1))
+                    nc.vector.scalar_tensor_tensor(
+                        out=zs[:, cols], in0=ow[i][:, cols], scalar=0.5, in1=zb[i, hd][:],
+                        op0=ALU.mult, op1=ALU.add, accum_out=sm[:],
+                    )
+                nc.vector.tensor_scalar(
+                    out=nm[:], in0=sm0[:], scalar1=sm1[:], scalar2=-1.0 / D, op0=ALU.add, op1=ALU.mult
+                )
+                nc.scalar.activation(out=junk[:], in_=zs[:], func=ACT.Square, bias=nm[:], accum_out=sq[:])
+                nc.scalar.activation(out=rs[i][:], in_=sq[:], func=ACT.Abs_reciprocal_sqrt, bias=EPS, scale=1.0 / D)
+                zs_[i] = zs
+                nmean[i] = nm
+
+        def centre(i):
+            q = work.tile([P, D], F32, name="q", bufs=3)
+            qt[i] = q
+            if i in OWN_ON_T:
+                for hd in range(2):
+                    cols = slice(512 * hd, 512 * (hd + 1))
+                    nc.vector.scalar_tensor_tensor(
+                        out=q[:, cols], in0=zb[i, hd][:], scalar=nmean[i][:, 0:1], in1=g_b[:, cols],
+                        op0=ALU.subtract, op1=ALU.mult,
+                    )
+            else:
+                nc.vector.scalar_tensor_tensor(
+                    out=q[:], in0=zs_[i][:], scalar=nmean[i][:], in1=g_b[:], op0=ALU.add, op1=ALU.mult
+                )
+
+        def leave(i):
+            q = qt[i]
+            if i == NB - 1:
+                o = q
+                for hd in range(2):
+                    cols = slice(512 * hd, 512 * (hd + 1))
+                    nc.vector.scalar_tensor_tensor(
+                        out=o[:, cols], in0=q[:, cols], scalar=rs[i][:], in1=be_b[:, cols], op0=ALU.mult, op1=ALU.add
+                    )
+                    nc.sync.dma_start(out=out[P * i : P * (i + 1), cols], in_=o[:, cols])
+                return
+            o = work.tile([P, D], F32, name="o", bufs=3)
+            nc.scalar.activation(out=q[:], in_=q[:], func=ACT.Copy, scale=rs[i][:])
+            nc.gpsimd.tensor_tensor(out=o[:], in0=q[:], in1=be_b[:], op=ALU.add)
+            nc.sync.dma_start(out=out[P * i : P * (i + 1), :], in_=o[:])
+
+        def cw(gg, tp):
+            quant(wvc, wvs, wvg[gg, tp], slice(512 * gg + 256 * tp, 512 * gg + 256 * (tp + 1)))
+
+        def cx(q):
+            quant(xc, xsca, xg[q], slice(256 * q, 256 * (q + 1)))
+
+        def cwo(jp):
+            quant(woc, wos, wog[jp], slice(256 * jp, 256 * (jp + 1)))
+
+        def tw(gg, tp):
+            turn_wv(gg, 2 * tp)
+            turn_wv(gg, 2 * tp + 1)
+
+        def d(i, gg):
+            stage1(i, gg)
+            bias_v(i, gg)
+
+        def s2(c, js):
+            for j in js:
+                stage2(c, j)
+
+        def dd(i):
+            for gg in range(2):
+                d(i, gg)
+
+        def wos_(js):
+            for j in js:
+                turn_wo(j)
+
+        def bo_col():
+            bot = psum.tile([P, P], BF16, name="bot", tag="ps")
+            nc.tensor.transpose(bot[:], bo_rows[:], id16[:])
+            nc.scalar.activation(out=boh[:], in_=bot[:, 0:8], func=ACT.Copy, scale=0.5)
+
+        tw(0, 0)
+        scale_x(0)
+        tw(0, 1)
+        scale_x(1)
+        turn_x(0)
+        turn_x(1)
+        scale_x(2)
+        cw(0, 0)
+        tw(1, 0)
+        scale_x(3)
+        cw(0, 1)
+        tw(1, 1)
+        cx(0)
+        cw(1, 0)
+        turn_x(2)
+        turn_x(3)
+        bo_col()
+        cx(1)
+        cw(1, 1)
+        scale_x(4)
+        scale_x(5)
+        dd(0)
+        dd(1)
+        quant_v(0)
+        turn_x(4)
+        turn_x(5)
+        wos_(range(0, 4))
+        dd(2)
+        dd(3)
+        quant_v(1)
+        scale_x(6)
+        cwo(0)
+        scale_x(7)
+        cwo(1)
+        cx(2)
+        wos_(range(4, 8))
+        turn_x(6)
+        turn_x(7)
+        cwo(2)
+        cwo(3)
+        cx(3)
+        s2(0, range(0, 8))
+        dd(4)
+        dd(5)
+        quant_v(2)
+        dd(6)
+        dd(7)
+        quant_v(3)
+        zsum(0)
+        zsum(1)
+        stats(0)
+        stats(1)
+        centre(0)
+        leave(0)
+        s2(1, range(0, 4))
+        zsum(2)
+        stats(2)
+        centre(1)
+        leave(1)
+        s2(1, range(4, 8))
+        for i in range(3, 8):
+            zsum(i)
+            stats(i)
+            centre(i - 1)
+            leave(i - 1)
+        centre(7)
+        leave(7)

@@ -18,7 +18,7 @@ P = 128
 D = 1024
 NB = 8
 EPS = 1e-5
-OWN_ON_T = ()
+OWN_ON_T = (0, 1, 2)
 
 
 def tile_efficientfusionlayer_pb_kernel(
@@ -29,12 +29,11 @@ def tile_efficientfusionlayer_pb_kernel(
         const = ctx.enter_context(tc.tile_pool(name="const", bufs=1))
         ring = ctx.enter_context(tc.tile_pool(name="ring", bufs=1))
         work = ctx.enter_context(tc.tile_pool(name="work", bufs=2))
-        psum = ctx.enter_context(tc.psum_pool(name="psum", bufs=8))
+        psum = ctx.enter_context(tc.psum_pool(name="psum", bufs=1))
 
         ctx.enter_context(tc.manual_schedule())
         sc = const.tile([P, D], F32, name="sc")
-        nc.scalar.dma_start(out=sc[:], in_=xscale.rearrange("o k -> (o k)").partition_broadcast(P))
-        wv_raw = [[ring.tile([P, 2, D], BF16, name=f"wv{gg}{tp}", tag="wraw", bufs=8) for tp in range(2)] for gg in range(2)]
+        wv_raw = [[ring.tile([P, 2, D], BF16, name=f"wv{gg}{tp}", tag="wraw", bufs=10) for tp in range(2)] for gg in range(2)]
         wvsrc = Wv.rearrange("(g m t) k -> g m t k", g=2, t=4)
         xb = [const.tile([P, 2, D], U8, name=f"xb{c}") for c in range(4)]
         xsrc = xbytes.rearrange("(c i p) k -> c p i k", c=4, i=2)
@@ -46,6 +45,7 @@ def tile_efficientfusionlayer_pb_kernel(
             nc.sync.dma_start(out=xb[c][:], in_=xsrc[c])
 
         load_wv(0, 0)
+        nc.sync.dma_start(out=sc[:], in_=xscale.rearrange("o k -> (o k)").partition_broadcast(P))
         load_x(0)
         load_wv(0, 1)
         load_x(1)
@@ -58,21 +58,24 @@ def tile_efficientfusionlayer_pb_kernel(
         bo_rows = const.tile([P, P], BF16, name="bo_rows")
         nc.gpsimd.memset(bo_rows[:], 0.0)
         nc.scalar.dma_start(out=bo_rows[0:8, :], in_=bo.rearrange("(j p) -> j p", p=P))
-        wo_raw = [ring.tile([P, 2, D], BF16, name=f"wo{jp}", tag="wraw", bufs=8) for jp in range(4)]
+        wo_raw = [ring.tile([P, 2, D], BF16, name=f"wo{jp}", tag="wraw", bufs=10) for jp in range(4)]
         wosrc = Wo.rearrange("(q j m) e -> q m j e", q=4, j=2)
         for jp in range(4):
             nc.sync.dma_start(out=wo_raw[jp][:], in_=wosrc[jp])
         g_b = const.tile([P, D], BF16, name="g_b")
         be_b = const.tile([P, D], BF16, name="be_b")
-        ft = [const.tile([P, D], BF16, name=f"ft{i}") for i in range(NB)]
-        ow = [const.tile([P, D], BF16, name=f"ow{i}") for i in range(NB)]
-        for i in range(NB):
-            nc.sync.dma_start(out=ft[i][:], in_=feat[P * i : P * (i + 1), :])
-            nc.sync.dma_start(out=ow[i][:], in_=own_self[P * i : P * (i + 1), :])
+        nc.sync.dma_start(out=g_b[:], in_=g.partition_broadcast(P))
+        fo = {}
+
+        def load_fo(i):
+            fo[i] = ring.tile([P, 2, D], BF16, name=f"fo{i}", tag="wraw", bufs=10)
+            nc.sync.dma_start(out=fo[i][:, 0, :], in_=feat[P * i : P * (i + 1), :])
+            nc.sync.dma_start(out=fo[i][:, 1, :], in_=own_self[P * i : P * (i + 1), :])
             if i == 1:
-                nc.sync.dma_start(out=g_b[:], in_=g.partition_broadcast(P))
                 nc.sync.dma_start(out=be_b[:], in_=be.partition_broadcast(P))
 
+        load_fo(0)
+        load_fo(1)
         id32 = const.tile([P, P], F32, name="id32")
         make_identity(nc, id32[:])
         id16 = const.tile([P, P], BF16, name="id16")
@@ -81,13 +84,8 @@ def tile_efficientfusionlayer_pb_kernel(
         nc.vector.tensor_scalar(out=ih16[:], in0=id32[:], scalar1=0.5, scalar2=None, op0=ALU.mult)
 
         xs = {}
-        xg = {}
-        wvg = {}
-        wog = {}
+        grouped = {}
         ct = {}
-
-        def grp(name):
-            return ring.tile([P, 2, 256, 2], F32, name=name, tag="grp", bufs=8, align_bytes=64)
 
         xc = const.tile([P, 2, D], U32, name="xc", align_bytes=64)
         xsca = const.tile([P, 2, D], U8, name="xsca", align_bytes=64)
@@ -100,13 +98,32 @@ def tile_efficientfusionlayer_pb_kernel(
         vs = const.tile([P, 2, D], U8, name="vs", align_bytes=64)
         boh = const.tile([P, 8], F32, name="boh")
 
-        def turn(rows, dst):
+        banks = {}
+
+        def t_turn(kind, n):
+            if kind == "x":
+                rows = xs[n][:]
+            elif kind == "w":
+                rows = wv_raw[n // 4][n // 2 % 2][:, n % 2, :]
+            else:
+                rows = wo_raw[n // 2][:, n % 2, :]
             words = rows.bitcast(F32)
-            bank = psum.tile([P, 2, 2, P], F32, name="tp", tag="ps")
+            tag = "g" if kind == "o" else "ps"
+            bank = psum.tile([P, 2, 2, P], F32, name="tp", tag=tag, bufs=2 if kind == "o" else 6)
             for h in range(2):
                 for u in range(2):
                     nc.tensor.transpose(bank[:, h, u, :], words[:, 256 * h + u : 256 * (h + 1) : 2], id32[:])
-            nc.scalar.copy(out=dst, in_=bank[:].rearrange("p h u r -> p h r u"))
+            banks[kind, n] = bank
+
+        def e_turn(kind, n):
+            if (kind, n // 2) not in grouped:
+                grouped[kind, n // 2] = ring.tile(
+                    [P, 2, 256, 2], F32, name=f"{kind}{n}", tag="grp", bufs=8, align_bytes=64
+                )
+            nc.scalar.copy(
+                out=grouped[kind, n // 2][:, :, P * (n % 2) : P * (n % 2 + 1), :],
+                in_=banks[kind, n][:].rearrange("p h u r -> p h r u"),
+            )
 
         def quant(codes, scales, grouped, cols):
             for h in range(2):
@@ -122,25 +139,10 @@ def tile_efficientfusionlayer_pb_kernel(
                 out=xs[i][:], in0=xb[i // 2][:, i % 2, :].bitcast(E4M3), in1=sc[:], op=ALU.mult
             )
 
-        def turn_x(i):
-            if i % 2 == 0:
-                xg[i // 2] = grp(f"xg{i}")
-            turn(xs[i][:], xg[i // 2][:, :, P * (i % 2) : P * (i % 2 + 1), :])
-
-        def turn_wv(gg, t):
-            if t % 2 == 0:
-                wvg[gg, t // 2] = grp(f"wvg{gg}{t}")
-            turn(wv_raw[gg][t // 2][:, t % 2, :], wvg[gg, t // 2][:, :, P * (t % 2) : P * (t % 2 + 1), :])
-
-        def turn_wo(j):
-            if j % 2 == 0:
-                wog[j // 2] = grp(f"wog{j}")
-            turn(wo_raw[j // 2][:, j % 2, :], wog[j // 2][:, :, P * (j % 2) : P * (j % 2 + 1), :])
-
         s1 = {}
 
         def stage1(i, gg):
-            bank = psum.tile([P, 4, P], F32, name="s1", tag="ps")
+            bank = psum.tile([P, 4, P], F32, name="s1", tag="ps", bufs=6)
             s1[i, gg] = bank
             for t in range(4):
                 lc = slice(512 * gg + P * t, 512 * gg + P * (t + 1))
@@ -157,7 +159,7 @@ def tile_efficientfusionlayer_pb_kernel(
                     )
 
         def bias_v(i, gg):
-            if i % 2 == 0:
+            if (i // 2, gg) not in vg:
                 vg[i // 2, gg] = ring.tile([P, 256, 4], BF16, name=f"vg{i}{gg}", tag="vg", bufs=5, align_bytes=64)
             nc.vector.tensor_tensor(
                 out=vg[i // 2, gg][:, P * (i % 2) : P * (i % 2 + 1), :],
@@ -175,8 +177,10 @@ def tile_efficientfusionlayer_pb_kernel(
                     in_=vg[q, gg][:].rearrange("p b t -> p (b t)"),
                 )
 
+        s2b = {}
+
         def stage2(c, j):
-            bank = psum.tile([P, 512], F32, name="s2", tag="ps")
+            bank = psum.tile([P, 512], F32, name="s2", tag="ps", bufs=6)
             ct[c, j] = ring.tile([P, 512], F32, name=f"ct{c}{j}", tag="ct", bufs=16)
             lc = slice(P * j, P * (j + 1))
             rc = slice(512 * c, 512 * (c + 1))
@@ -190,18 +194,23 @@ def tile_efficientfusionlayer_pb_kernel(
                     start=(gg == 0),
                     stop=(gg == 1),
                 )
-            nc.scalar.activation(out=ct[c, j][:], in_=bank[:], func=ACT.Identity, bias=boh[:, j : j + 1], scale=0.5)
+            s2b[c, j] = bank
+
+        def cross_out(c, j):
+            nc.scalar.activation(
+                out=ct[c, j][:], in_=s2b[c, j][:], func=ACT.Identity, bias=boh[:, j : j + 1], scale=0.5
+            )
 
         zb, zs_, qt, rs, nmean = {}, {}, {}, {}, {}
 
         def zsum(i):
             c, sl = i // 4, slice(P * (i % 4), P * (i % 4 + 1))
             for hd in range(2):
-                z = psum.tile([P, 512], F32, name="z", tag="ps")
+                z = psum.tile([P, 512], F32, name="z", tag="ps", bufs=6)
                 cols = slice(512 * hd, 512 * (hd + 1))
-                nc.tensor.matmul(out=z[:], lhsT=id16[:], rhs=ft[i][:, cols], start=True, stop=False)
+                nc.tensor.matmul(out=z[:], lhsT=id16[:], rhs=fo[i][:, 0, cols], start=True, stop=False)
                 if i in OWN_ON_T:
-                    nc.tensor.matmul(out=z[:], lhsT=ih16[:], rhs=ow[i][:, cols], start=False, stop=False)
+                    nc.tensor.matmul(out=z[:], lhsT=ih16[:], rhs=fo[i][:, 1, cols], start=False, stop=False)
                 zb[i, hd] = z
             for hd in range(2):
                 for jj in range(4):
@@ -215,38 +224,42 @@ def tile_efficientfusionlayer_pb_kernel(
                     )
 
         def stats(i):
-            rs[i] = work.tile([P, 1], F32, name="rstd")
+            rs[i] = work.tile([P, 1], F32, name="rstd", bufs=8)
             if i in OWN_ON_T:
-                st = work.tile([P, 2, 6], F32, name="st")
-                mv = work.tile([P, 2], F32, name="mv")
+                st = work.tile([P, 2, 6], F32, name="st", bufs=4)
+                mv = work.tile([P, 2], F32, name="mv", bufs=8)
                 for hd in range(2):
                     nc.vector.bn_stats(out=st[:, hd, :], in_=zb[i, hd][:])
                 nc.vector.bn_aggr(out=mv[:], in_=st[:].rearrange("p a b -> p (a b)"))
-                nc.scalar.activation(out=rs[i][:], in_=mv[:, 1:2], func=ACT.Abs_reciprocal_sqrt, bias=EPS)
                 nmean[i] = mv
             else:
-                zs = work.tile([P, D], F32, name="zs")
-                sm0 = work.tile([P, 1], F32, name="sm0")
-                sm1 = work.tile([P, 1], F32, name="sm1")
-                nm = work.tile([P, 1], F32, name="nm")
-                sq = work.tile([P, 1], F32, name="sq")
-                junk = work.tile([P, D], BF16, name="junk", bufs=1)
+                zs = work.tile([P, D], F32, name="zs", bufs=3)
+                sm0 = work.tile([P, 1], F32, name="sm0", bufs=8)
+                sm1 = work.tile([P, 1], F32, name="sm1", bufs=8)
+                nm = work.tile([P, 1], F32, name="nm", bufs=8)
                 for hd, sm in ((0, sm0), (1, sm1)):
                     cols = slice(512 * hd, 512 * (hd + 1))
                     nc.vector.scalar_tensor_tensor(
-                        out=zs[:, cols], in0=ow[i][:, cols], scalar=0.5, in1=zb[i, hd][:],
+                        out=zs[:, cols], in0=fo[i][:, 1, cols], scalar=0.5, in1=zb[i, hd][:],
                         op0=ALU.mult, op1=ALU.add, accum_out=sm[:],
                     )
                 nc.vector.tensor_scalar(
                     out=nm[:], in0=sm0[:], scalar1=sm1[:], scalar2=-1.0 / D, op0=ALU.add, op1=ALU.mult
                 )
-                nc.scalar.activation(out=junk[:], in_=zs[:], func=ACT.Square, bias=nm[:], accum_out=sq[:])
-                nc.scalar.activation(out=rs[i][:], in_=sq[:], func=ACT.Abs_reciprocal_sqrt, bias=EPS, scale=1.0 / D)
                 zs_[i] = zs
                 nmean[i] = nm
 
+        def spread(i):
+            if i in OWN_ON_T:
+                nc.scalar.activation(out=rs[i][:], in_=nmean[i][:, 1:2], func=ACT.Abs_reciprocal_sqrt, bias=EPS)
+                return
+            sq = work.tile([P, 1], F32, name="sq", bufs=8)
+            junk = work.tile([P, D], BF16, name="junk", bufs=1)
+            nc.scalar.activation(out=junk[:], in_=zs_[i][:], func=ACT.Square, bias=nmean[i][:], accum_out=sq[:])
+            nc.scalar.activation(out=rs[i][:], in_=sq[:], func=ACT.Abs_reciprocal_sqrt, bias=EPS, scale=1.0 / D)
+
         def centre(i):
-            q = work.tile([P, D], F32, name="q", bufs=3)
+            q = work.tile([P, D], F32, name="q", bufs=4)
             qt[i] = q
             if i in OWN_ON_T:
                 for hd in range(2):
@@ -256,124 +269,254 @@ def tile_efficientfusionlayer_pb_kernel(
                         op0=ALU.subtract, op1=ALU.mult,
                     )
             else:
-                nc.vector.scalar_tensor_tensor(
-                    out=q[:], in0=zs_[i][:], scalar=nmean[i][:], in1=g_b[:], op0=ALU.add, op1=ALU.mult
-                )
-
-        def leave(i):
-            q = qt[i]
-            if i == NB - 1:
-                o = q
                 for hd in range(2):
                     cols = slice(512 * hd, 512 * (hd + 1))
                     nc.vector.scalar_tensor_tensor(
-                        out=o[:, cols], in0=q[:, cols], scalar=rs[i][:], in1=be_b[:, cols], op0=ALU.mult, op1=ALU.add
+                        out=q[:, cols], in0=zs_[i][:, cols], scalar=nmean[i][:], in1=g_ps[hd][:],
+                        op0=ALU.add, op1=ALU.mult,
                     )
-                    nc.sync.dma_start(out=out[P * i : P * (i + 1), cols], in_=o[:, cols])
-                return
+
+        g_ps = []
+
+        def g_bank():
+            for hd in range(2):
+                bank = psum.tile([P, 512], F32, name="gb", tag="g", bufs=2)
+                nc.tensor.matmul(
+                    out=bank[:], lhsT=id16[:], rhs=g_b[:, 512 * hd : 512 * (hd + 1)], start=True, stop=True
+                )
+                g_ps.append(bank)
+
+        def leave_v(i):
+            q = qt[i]
+            for hd in range(2):
+                cols = slice(512 * hd, 512 * (hd + 1))
+                nc.vector.scalar_tensor_tensor(
+                    out=q[:, cols], in0=q[:, cols], scalar=rs[i][:], in1=be_b[:, cols], op0=ALU.mult, op1=ALU.add
+                )
+                nc.sync.dma_start(out=out[P * i : P * (i + 1), cols], in_=q[:, cols])
+
+        def norm(i):
+            nc.scalar.activation(out=qt[i][:], in_=qt[i][:], func=ACT.Copy, scale=rs[i][:])
+
+        def leave_g(i):
             o = work.tile([P, D], F32, name="o", bufs=3)
-            nc.scalar.activation(out=q[:], in_=q[:], func=ACT.Copy, scale=rs[i][:])
-            nc.gpsimd.tensor_tensor(out=o[:], in0=q[:], in1=be_b[:], op=ALU.add)
+            nc.gpsimd.tensor_tensor(out=o[:], in0=qt[i][:], in1=be_b[:], op=ALU.add)
             nc.sync.dma_start(out=out[P * i : P * (i + 1), :], in_=o[:])
 
         def cw(gg, tp):
-            quant(wvc, wvs, wvg[gg, tp], slice(512 * gg + 256 * tp, 512 * gg + 256 * (tp + 1)))
+            quant(wvc, wvs, grouped["w", 2 * gg + tp], slice(512 * gg + 256 * tp, 512 * gg + 256 * (tp + 1)))
 
         def cx(q):
-            quant(xc, xsca, xg[q], slice(256 * q, 256 * (q + 1)))
+            quant(xc, xsca, grouped["x", q], slice(256 * q, 256 * (q + 1)))
 
         def cwo(jp):
-            quant(woc, wos, wog[jp], slice(256 * jp, 256 * (jp + 1)))
+            quant(woc, wos, grouped["o", jp], slice(256 * jp, 256 * (jp + 1)))
 
-        def tw(gg, tp):
-            turn_wv(gg, 2 * tp)
-            turn_wv(gg, 2 * tp + 1)
+        def cw(n):
+            quant(wvc, wvs, grouped["w", n], slice(256 * n, 256 * (n + 1)))
 
-        def d(i, gg):
-            stage1(i, gg)
-            bias_v(i, gg)
+        def cx(q):
+            quant(xc, xsca, grouped["x", q], slice(256 * q, 256 * (q + 1)))
 
-        def s2(c, js):
-            for j in js:
-                stage2(c, j)
+        def cwo(jp):
+            quant(woc, wos, grouped["o", jp], slice(256 * jp, 256 * (jp + 1)))
 
-        def dd(i):
-            for gg in range(2):
-                d(i, gg)
+        def bo_t():
+            banks["b", 0] = psum.tile([P, P], BF16, name="bot", tag="ps", bufs=6)
+            nc.tensor.transpose(banks["b", 0][:], bo_rows[:], id16[:])
 
-        def wos_(js):
-            for j in js:
-                turn_wo(j)
+        def bo_e():
+            nc.scalar.activation(out=boh[:], in_=banks["b", 0][:, 0:8], func=ACT.Copy, scale=0.5)
 
-        def bo_col():
-            bot = psum.tile([P, P], BF16, name="bot", tag="ps")
-            nc.tensor.transpose(bot[:], bo_rows[:], id16[:])
-            nc.scalar.activation(out=boh[:], in_=bot[:, 0:8], func=ACT.Copy, scale=0.5)
-
-        tw(0, 0)
         scale_x(0)
-        tw(0, 1)
+        t_turn("w", 0)
+        t_turn("w", 1)
+        t_turn("x", 0)
+        e_turn("w", 0)
+        t_turn("w", 2)
         scale_x(1)
-        turn_x(0)
-        turn_x(1)
-        scale_x(2)
-        cw(0, 0)
-        tw(1, 0)
+        e_turn("w", 1)
+        t_turn("w", 3)
+        t_turn("w", 5)
+        e_turn("x", 0)
+        t_turn("x", 1)
+        e_turn("w", 2)
+        e_turn("w", 5)
+        t_turn("w", 6)
+        e_turn("w", 3)
         scale_x(3)
-        cw(0, 1)
-        tw(1, 1)
-        cx(0)
-        cw(1, 0)
-        turn_x(2)
-        turn_x(3)
-        bo_col()
-        cx(1)
-        cw(1, 1)
+        scale_x(2)
+        e_turn("w", 6)
+        t_turn("x", 3)
         scale_x(4)
+        t_turn("w", 7)
+        t_turn("x", 2)
+        e_turn("x", 1)
+        e_turn("x", 3)
+        t_turn("x", 4)
+        e_turn("w", 7)
+        t_turn("w", 4)
+        load_fo(2)
+        load_fo(3)
+        load_fo(4)
+        load_fo(5)
         scale_x(5)
-        dd(0)
-        dd(1)
-        quant_v(0)
-        turn_x(4)
-        turn_x(5)
-        wos_(range(0, 4))
-        dd(2)
-        dd(3)
-        quant_v(1)
-        scale_x(6)
-        cwo(0)
+        t_turn("o", 1)
+        e_turn("x", 2)
+        cw(0)
+        e_turn("o", 1)
+        cw(1)
+        cx(0)
+        cx(1)
+        e_turn("w", 4)
+        t_turn("o", 0)
+        t_turn("x", 5)
+        t_turn("o", 2)
+        e_turn("o", 0)
+        e_turn("x", 4)
+        bo_t()
+        e_turn("x", 5)
+        bo_e()
+        cw(3)
+        stage1(1, 0)
+        t_turn("o", 7)
+        stage1(2, 0)
+        cw(2)
+        stage1(3, 0)
+        stage1(0, 1)
+        bias_v(1, 0)
+        stage1(1, 1)
         scale_x(7)
-        cwo(1)
+        stage1(0, 0)
+        stage1(2, 1)
+        bias_v(2, 0)
+        e_turn("o", 2)
+        e_turn("o", 7)
+        stage1(3, 1)
+        t_turn("o", 6)
+        bias_v(3, 0)
+        scale_x(6)
+        bias_v(0, 1)
         cx(2)
-        wos_(range(4, 8))
-        turn_x(6)
-        turn_x(7)
-        cwo(2)
+        bias_v(0, 0)
+        t_turn("o", 4)
+        t_turn("x", 7)
+        e_turn("o", 6)
+        e_turn("o", 4)
+        bias_v(3, 1)
+        bias_v(2, 1)
+        t_turn("o", 5)
+        bias_v(1, 1)
+        quant_v(1)
+        t_turn("o", 3)
+        load_fo(6)
+        load_fo(7)
+        cwo(0)
+        t_turn("x", 6)
+        e_turn("o", 5)
+        stage1(4, 0)
+        stage1(5, 1)
+        e_turn("x", 7)
         cwo(3)
+        quant_v(0)
+        stage1(4, 1)
+        e_turn("x", 6)
         cx(3)
-        s2(0, range(0, 8))
-        dd(4)
-        dd(5)
+        e_turn("o", 3)
+        g_bank()
+        stage2(0, 6)
+        bias_v(4, 1)
+        cross_out(0, 6)
+        stage2(0, 1)
+        cross_out(0, 1)
+        stage2(0, 0)
+        bias_v(4, 0)
+        stage2(0, 7)
+        bias_v(5, 1)
+        cross_out(0, 7)
+        cross_out(0, 0)
+        stage1(5, 0)
+        cwo(1)
+        stage2(0, 2)
+        stage2(0, 3)
+        cwo(2)
+        cross_out(0, 2)
+        cross_out(0, 3)
+        stage1(6, 1)
+        stage1(7, 1)
+        stage2(0, 5)
+        bias_v(5, 0)
         quant_v(2)
-        dd(6)
-        dd(7)
-        quant_v(3)
+        stage2(0, 4)
+        bias_v(6, 1)
+        cross_out(0, 5)
+        cross_out(0, 4)
+        bias_v(7, 1)
+        stage1(7, 0)
+        stage1(6, 0)
+        bias_v(7, 0)
         zsum(0)
-        zsum(1)
+        bias_v(6, 0)
+        quant_v(3)
+        stage2(1, 7)
         stats(0)
-        stats(1)
         centre(0)
-        leave(0)
-        s2(1, range(0, 4))
+        stage2(1, 4)
+        zsum(1)
+        cross_out(1, 7)
+        stage2(1, 6)
+        stats(1)
+        cross_out(1, 4)
+        stage2(1, 2)
         zsum(2)
-        stats(2)
         centre(1)
-        leave(1)
-        s2(1, range(4, 8))
-        for i in range(3, 8):
-            zsum(i)
-            stats(i)
-            centre(i - 1)
-            leave(i - 1)
+        spread(0)
+        stats(2)
+        centre(2)
+        norm(0)
+        spread(1)
+        cross_out(1, 2)
+        norm(1)
+        zsum(3)
+        cross_out(1, 6)
+        stage2(1, 3)
+        stage2(1, 0)
+        stage2(1, 5)
+        spread(2)
+        cross_out(1, 3)
+        stage2(1, 1)
+        cross_out(1, 0)
+        cross_out(1, 5)
+        leave_g(0)
+        cross_out(1, 1)
+        stats(3)
+        zsum(4)
+        norm(2)
+        zsum(5)
+        centre(3)
+        spread(3)
+        stats(4)
+        leave_g(1)
+        zsum(6)
+        stats(5)
+        norm(3)
+        spread(4)
+        centre(5)
+        spread(5)
+        norm(5)
+        stats(6)
+        zsum(7)
+        centre(4)
+        leave_g(2)
+        leave_g(3)
+        spread(6)
+        stats(7)
+        leave_g(5)
+        centre(6)
         centre(7)
-        leave(7)
+        norm(4)
+        spread(7)
+        norm(6)
+        leave_g(4)
+        leave_v(7)
+        leave_g(6)

@@ -18,7 +18,8 @@ P = 128
 D = 1024
 NB = 8
 EPS = 1e-5
-OWN_ON_T = (0, 1, 2)
+OWN_ON_T = ()
+NORM_ON_G = (0, 1)
 
 
 def tile_efficientfusionlayer_pb_kernel(
@@ -33,6 +34,10 @@ def tile_efficientfusionlayer_pb_kernel(
 
         ctx.enter_context(tc.manual_schedule())
         sc = const.tile([P, D], F32, name="sc")
+        s_rows = const.tile([P, P], F32, name="s_rows")
+        nc.gpsimd.memset(s_rows[:], 0.0)
+        nc.scalar.dma_start(out=s_rows[0:8, :], in_=xscale.rearrange("o (c p) -> (o c) p", p=P))
+        s_col = const.tile([P, 8], F32, name="s_col")
         wv_raw = [[ring.tile([P, 2, D], BF16, name=f"wv{gg}{tp}", tag="wraw", bufs=10) for tp in range(2)] for gg in range(2)]
         wvsrc = Wv.rearrange("(g m t) k -> g m t k", g=2, t=4)
         xb = [const.tile([P, 2, D], U8, name=f"xb{c}") for c in range(4)]
@@ -45,7 +50,6 @@ def tile_efficientfusionlayer_pb_kernel(
             nc.sync.dma_start(out=xb[c][:], in_=xsrc[c])
 
         load_wv(0, 0)
-        nc.sync.dma_start(out=sc[:], in_=xscale.rearrange("o k -> (o k)").partition_broadcast(P))
         load_x(0)
         load_wv(0, 1)
         load_x(1)
@@ -160,12 +164,47 @@ def tile_efficientfusionlayer_pb_kernel(
 
         def bias_v(i, gg):
             if (i // 2, gg) not in vg:
-                vg[i // 2, gg] = ring.tile([P, 256, 4], BF16, name=f"vg{i}{gg}", tag="vg", bufs=5, align_bytes=64)
+                vg[i // 2, gg] = ring.tile([P, 256, 4], BF16, name=f"vg{i}{gg}", tag="vg", bufs=4, align_bytes=64)
             nc.vector.tensor_tensor(
                 out=vg[i // 2, gg][:, P * (i % 2) : P * (i % 2 + 1), :],
                 in0=s1[i, gg][:].rearrange("p t b -> p b t"),
                 in1=bv_t[:, gg, :].unsqueeze(1).to_broadcast([P, P, 4]),
                 op=ALU.add,
+            )
+
+        n1, vp = {}, {}
+
+        def stage1_pair(q, gg, u):
+            bank = psum.tile([P, 2, 256], F32, name="n1", tag="ps", bufs=6)
+            n1[q, gg, u] = bank
+            rc = slice(256 * q, 256 * (q + 1))
+            for a in range(2):
+                lc = slice(512 * gg + P * (2 * u + a), 512 * gg + P * (2 * u + a + 1))
+                for h in range(2):
+                    nc.tensor.matmul_mx(
+                        out=bank[:, a, :],
+                        lhsT=wvc[:, h, lc].bitcast(X4),
+                        lhsT_scale=wvs[:, h, lc],
+                        rhs=xc[:, h, rc].bitcast(X4),
+                        rhs_scale=xsca[:, h, rc],
+                        start=(h == 0),
+                        stop=(h == 1),
+                    )
+
+        def bias_s(q, gg, u):
+            if (q, gg) not in vp:
+                vp[q, gg] = ring.tile([P, 4, 256], BF16, name=f"vp{q}{gg}", tag="vp", bufs=2, align_bytes=64)
+            for a in range(2):
+                t = 2 * u + a
+                nc.scalar.activation(
+                    out=vp[q, gg][:, t, :], in_=n1[q, gg, u][:, a, :], func=ACT.Identity, bias=bv_t[:, gg, t : t + 1]
+                )
+
+        def interleave(q, gg):
+            vg[q, gg] = ring.tile([P, 256, 4], BF16, name=f"vg{q}{gg}", tag="vg", bufs=4, align_bytes=64)
+            nc.vector.tensor_copy(
+                out=vg[q, gg][:].rearrange("p (c i) t -> p c t i", i=4),
+                in_=vp[q, gg][:].rearrange("p t (c i) -> p c t i", i=4),
             )
 
         def quant_v(q):
@@ -179,32 +218,35 @@ def tile_efficientfusionlayer_pb_kernel(
 
         s2b = {}
 
-        def stage2(c, j):
-            bank = psum.tile([P, 512], F32, name="s2", tag="ps", bufs=6)
-            ct[c, j] = ring.tile([P, 512], F32, name=f"ct{c}{j}", tag="ct", bufs=16)
-            lc = slice(P * j, P * (j + 1))
-            rc = slice(512 * c, 512 * (c + 1))
-            for gg in range(2):
-                nc.tensor.matmul_mx(
-                    out=bank[:],
-                    lhsT=woc[:, gg, lc].bitcast(X4),
-                    lhsT_scale=wos[:, gg, lc],
-                    rhs=vc[:, gg, rc].bitcast(X4),
-                    rhs_scale=vs[:, gg, rc],
-                    start=(gg == 0),
-                    stop=(gg == 1),
-                )
-            s2b[c, j] = bank
+        def stage2(q, jj):
+            bank = psum.tile([P, 2, 256], F32, name="s2", tag="ps", bufs=6)
+            s2b[q, jj] = bank
+            ct[q, jj] = ring.tile([P, 2, 256], F32, name=f"ct{q}{jj}", tag="ct", bufs=16)
+            rc = slice(256 * q, 256 * (q + 1))
+            for a in range(2):
+                lc = slice(P * (2 * jj + a), P * (2 * jj + a + 1))
+                for gg in range(2):
+                    nc.tensor.matmul_mx(
+                        out=bank[:, a, :],
+                        lhsT=woc[:, gg, lc].bitcast(X4),
+                        lhsT_scale=wos[:, gg, lc],
+                        rhs=vc[:, gg, rc].bitcast(X4),
+                        rhs_scale=vs[:, gg, rc],
+                        start=(gg == 0),
+                        stop=(gg == 1),
+                    )
 
-        def cross_out(c, j):
-            nc.scalar.activation(
-                out=ct[c, j][:], in_=s2b[c, j][:], func=ACT.Identity, bias=boh[:, j : j + 1], scale=0.5
-            )
+        def cross_out(q, jj):
+            for a in range(2):
+                j = 2 * jj + a
+                nc.scalar.activation(
+                    out=ct[q, jj][:, a, :], in_=s2b[q, jj][:, a, :], func=ACT.Identity, bias=boh[:, j : j + 1], scale=0.5
+                )
 
         zb, zs_, qt, rs, nmean = {}, {}, {}, {}, {}
 
         def zsum(i):
-            c, sl = i // 4, slice(P * (i % 4), P * (i % 4 + 1))
+            sl = slice(P * (i % 2), P * (i % 2 + 1))
             for hd in range(2):
                 z = psum.tile([P, 512], F32, name="z", tag="ps", bufs=6)
                 cols = slice(512 * hd, 512 * (hd + 1))
@@ -216,7 +258,7 @@ def tile_efficientfusionlayer_pb_kernel(
                 for jj in range(4):
                     nc.tensor.matmul(
                         out=zb[i, hd][:, P * jj : P * (jj + 1)],
-                        lhsT=ct[c, 4 * hd + jj][:, sl],
+                        lhsT=ct[i // 2, 2 * hd + jj // 2][:, jj % 2, sl],
                         rhs=id32[:],
                         start=False,
                         stop=(jj == 3),
@@ -296,10 +338,18 @@ def tile_efficientfusionlayer_pb_kernel(
                 nc.sync.dma_start(out=out[P * i : P * (i + 1), cols], in_=q[:, cols])
 
         def norm(i):
+            if i in NORM_ON_G:
+                qt[i] = work.tile([P, D], F32, name="q", bufs=4)
+                shift = work.tile([P, 1], F32, name="shift", bufs=8)
+                nc.scalar.activation(out=shift[:], in_=nmean[i][:], func=ACT.Copy, scale=rs[i][:])
+                nc.scalar.activation(out=qt[i][:], in_=zs_[i][:], func=ACT.Identity, bias=shift[:], scale=rs[i][:])
+                return
             nc.scalar.activation(out=qt[i][:], in_=qt[i][:], func=ACT.Copy, scale=rs[i][:])
 
         def leave_g(i):
             o = work.tile([P, D], F32, name="o", bufs=3)
+            if i in NORM_ON_G:
+                nc.gpsimd.tensor_tensor(out=qt[i][:], in0=qt[i][:], in1=g_b[:], op=ALU.mult)
             nc.gpsimd.tensor_tensor(out=o[:], in0=qt[i][:], in1=be_b[:], op=ALU.add)
             nc.sync.dma_start(out=out[P * i : P * (i + 1), :], in_=o[:])
 
@@ -321,6 +371,25 @@ def tile_efficientfusionlayer_pb_kernel(
         def cwo(jp):
             quant(woc, wos, grouped["o", jp], slice(256 * jp, 256 * (jp + 1)))
 
+        def s_turn():
+            banks["s", 0] = psum.tile([P, P], F32, name="st0", tag="ps", bufs=6)
+            nc.tensor.transpose(banks["s", 0][:], s_rows[:], id32[:])
+
+        def s_cols():
+            nc.scalar.copy(out=s_col[:], in_=banks["s", 0][:, 0:8])
+
+        def s_spread(hd):
+            bank = psum.tile([P, 4, P], F32, name="sb", tag="ps", bufs=6)
+            for c in range(4):
+                nc.tensor.transpose(
+                    bank[:, c, :], s_col[:, 4 * hd + c : 4 * hd + c + 1].to_broadcast([P, P]), id32[:]
+                )
+            banks["sb", hd] = bank
+
+        def s_out(hd):
+            copy = nc.vector.tensor_copy if hd else nc.scalar.copy
+            copy(out=sc[:, 512 * hd : 512 * (hd + 1)], in_=banks["sb", hd][:].rearrange("p c k -> p (c k)"))
+
         def bo_t():
             banks["b", 0] = psum.tile([P, P], BF16, name="bot", tag="ps", bufs=6)
             nc.tensor.transpose(banks["b", 0][:], bo_rows[:], id16[:])
@@ -328,195 +397,198 @@ def tile_efficientfusionlayer_pb_kernel(
         def bo_e():
             nc.scalar.activation(out=boh[:], in_=banks["b", 0][:, 0:8], func=ACT.Copy, scale=0.5)
 
-        scale_x(0)
-        t_turn("w", 0)
+        s_turn()
+        s_cols()
+        s_spread(0)
+        s_spread(1)
+        s_out(0)
         t_turn("w", 1)
-        t_turn("x", 0)
-        e_turn("w", 0)
-        t_turn("w", 2)
-        scale_x(1)
+        s_out(1)
+        t_turn("w", 0)
         e_turn("w", 1)
+        scale_x(1)
+        t_turn("w", 2)
+        e_turn("w", 0)
         t_turn("w", 3)
-        t_turn("w", 5)
-        e_turn("x", 0)
+        scale_x(0)
         t_turn("x", 1)
-        e_turn("w", 2)
-        e_turn("w", 5)
-        t_turn("w", 6)
         e_turn("w", 3)
-        scale_x(3)
-        scale_x(2)
-        e_turn("w", 6)
-        t_turn("x", 3)
-        scale_x(4)
-        t_turn("w", 7)
-        t_turn("x", 2)
+        t_turn("w", 5)
         e_turn("x", 1)
-        e_turn("x", 3)
-        t_turn("x", 4)
-        e_turn("w", 7)
+        scale_x(2)
+        t_turn("x", 0)
+        e_turn("w", 2)
         t_turn("w", 4)
+        e_turn("x", 0)
+        scale_x(3)
+        t_turn("w", 6)
+        e_turn("w", 4)
+        t_turn("w", 7)
         load_fo(2)
         load_fo(3)
         load_fo(4)
         load_fo(5)
-        scale_x(5)
-        t_turn("o", 1)
-        e_turn("x", 2)
-        cw(0)
-        e_turn("o", 1)
+        e_turn("w", 6)
+        e_turn("w", 5)
         cw(1)
-        cx(0)
-        cx(1)
-        e_turn("w", 4)
         t_turn("o", 0)
-        t_turn("x", 5)
-        t_turn("o", 2)
+        t_turn("x", 3)
+        cw(0)
         e_turn("o", 0)
-        e_turn("x", 4)
-        bo_t()
-        e_turn("x", 5)
-        bo_e()
-        cw(3)
-        stage1(1, 0)
-        t_turn("o", 7)
-        stage1(2, 0)
-        cw(2)
-        stage1(3, 0)
-        stage1(0, 1)
-        bias_v(1, 0)
-        stage1(1, 1)
-        scale_x(7)
-        stage1(0, 0)
-        stage1(2, 1)
-        bias_v(2, 0)
-        e_turn("o", 2)
-        e_turn("o", 7)
-        stage1(3, 1)
-        t_turn("o", 6)
-        bias_v(3, 0)
-        scale_x(6)
-        bias_v(0, 1)
-        cx(2)
-        bias_v(0, 0)
-        t_turn("o", 4)
-        t_turn("x", 7)
-        e_turn("o", 6)
-        e_turn("o", 4)
-        bias_v(3, 1)
-        bias_v(2, 1)
-        t_turn("o", 5)
-        bias_v(1, 1)
-        quant_v(1)
+        t_turn("o", 1)
+        scale_x(4)
+        t_turn("x", 2)
+        e_turn("o", 1)
         t_turn("o", 3)
+        e_turn("w", 7)
+        cx(0)
+        t_turn("o", 4)
+        e_turn("o", 3)
+        t_turn("x", 4)
+        e_turn("o", 4)
+        cw(3)
+        t_turn("o", 7)
+        e_turn("x", 2)
+        stage1(1, 0)
+        cwo(0)
+        e_turn("x", 3)
+        scale_x(5)
+        stage1(0, 0)
+        e_turn("o", 7)
+        e_turn("x", 4)
+        cx(1)
+        cw(2)
+        bias_v(1, 0)
+        t_turn("o", 5)
+        bias_v(0, 0)
+        bo_t()
+        stage1(1, 1)
+        bo_e()
+        e_turn("o", 5)
+        t_turn("o", 6)
+        cwo(2)
+        stage1(2, 0)
+        stage1(0, 1)
+        stage1(2, 1)
+        scale_x(6)
+        bias_v(1, 1)
+        bias_v(2, 0)
+        t_turn("o", 2)
         load_fo(6)
         load_fo(7)
-        cwo(0)
-        t_turn("x", 6)
-        e_turn("o", 5)
-        stage1(4, 0)
-        stage1(5, 1)
-        e_turn("x", 7)
-        cwo(3)
+        bias_v(2, 1)
+        t_turn("x", 5)
+        bias_v(0, 1)
+        stage1(3, 1)
+        e_turn("x", 5)
         quant_v(0)
-        stage1(4, 1)
-        e_turn("x", 6)
-        cx(3)
-        e_turn("o", 3)
-        g_bank()
-        stage2(0, 6)
-        bias_v(4, 1)
-        cross_out(0, 6)
-        stage2(0, 1)
-        cross_out(0, 1)
-        stage2(0, 0)
-        bias_v(4, 0)
-        stage2(0, 7)
-        bias_v(5, 1)
-        cross_out(0, 7)
-        cross_out(0, 0)
-        stage1(5, 0)
+        e_turn("o", 2)
+        e_turn("o", 6)
+        stage1(3, 0)
+        cx(2)
         cwo(1)
         stage2(0, 2)
-        stage2(0, 3)
-        cwo(2)
+        stage2(0, 0)
+        bias_v(3, 0)
+        stage1(5, 0)
         cross_out(0, 2)
-        cross_out(0, 3)
-        stage1(6, 1)
-        stage1(7, 1)
-        stage2(0, 5)
+        bias_v(3, 1)
+        stage2(0, 1)
+        cross_out(0, 0)
+        cwo(3)
+        stage1(4, 0)
+        cross_out(0, 1)
+        quant_v(1)
         bias_v(5, 0)
-        quant_v(2)
-        stage2(0, 4)
-        bias_v(6, 1)
-        cross_out(0, 5)
-        cross_out(0, 4)
-        bias_v(7, 1)
-        stage1(7, 0)
-        stage1(6, 0)
-        bias_v(7, 0)
-        zsum(0)
-        bias_v(6, 0)
-        quant_v(3)
-        stage2(1, 7)
-        stats(0)
-        centre(0)
-        stage2(1, 4)
-        zsum(1)
-        cross_out(1, 7)
-        stage2(1, 6)
-        stats(1)
-        cross_out(1, 4)
-        stage2(1, 2)
-        zsum(2)
-        centre(1)
-        spread(0)
-        stats(2)
-        centre(2)
-        norm(0)
-        spread(1)
-        cross_out(1, 2)
-        norm(1)
-        zsum(3)
-        cross_out(1, 6)
+        stage1(5, 1)
+        stage2(0, 3)
+        bias_v(4, 0)
         stage2(1, 3)
-        stage2(1, 0)
-        stage2(1, 5)
-        spread(2)
-        cross_out(1, 3)
+        cross_out(0, 3)
+        bias_v(5, 1)
+        stage1(4, 1)
+        scale_x(7)
         stage2(1, 1)
-        cross_out(1, 0)
-        cross_out(1, 5)
-        leave_g(0)
+        zsum(0)
         cross_out(1, 1)
+        bias_v(4, 1)
+        cross_out(1, 3)
+        stage2(1, 2)
+        stats(0)
+        stage2(1, 0)
+        cross_out(1, 2)
+        g_bank()
+        cross_out(1, 0)
+        quant_v(2)
+        zsum(1)
+        spread(0)
+        t_turn("x", 7)
+        stats(1)
+        norm(0)
+        zsum(2)
+        e_turn("x", 7)
+        leave_g(0)
+        zsum(3)
+        spread(1)
+        stats(2)
+        t_turn("x", 6)
+        norm(1)
         stats(3)
-        zsum(4)
-        norm(2)
-        zsum(5)
+        stage2(2, 3)
+        stage2(2, 1)
+        e_turn("x", 6)
+        stage2(2, 2)
+        cross_out(2, 1)
+        cx(3)
+        stage2(2, 0)
+        cross_out(2, 2)
         centre(3)
-        spread(3)
-        stats(4)
         leave_g(1)
-        zsum(6)
-        stats(5)
+        stage1(6, 1)
+        cross_out(2, 3)
+        cross_out(2, 0)
+        stage1(6, 0)
+        spread(3)
+        stage1(7, 0)
+        stage1(7, 1)
+        bias_v(6, 1)
+        bias_v(6, 0)
+        zsum(4)
+        spread(2)
+        bias_v(7, 0)
+        bias_v(7, 1)
+        centre(2)
         norm(3)
-        spread(4)
+        zsum(5)
+        quant_v(3)
+        stats(4)
+        norm(2)
+        leave_g(3)
+        stage2(3, 1)
+        stage2(3, 0)
+        cross_out(3, 1)
+        stats(5)
+        stage2(3, 3)
+        cross_out(3, 0)
+        stage2(3, 2)
+        cross_out(3, 3)
+        leave_g(2)
+        cross_out(3, 2)
         centre(5)
         spread(5)
-        norm(5)
-        stats(6)
-        zsum(7)
+        zsum(6)
         centre(4)
-        leave_g(2)
-        leave_g(3)
-        spread(6)
-        stats(7)
-        leave_g(5)
+        spread(4)
+        zsum(7)
+        stats(6)
+        norm(5)
         centre(6)
-        centre(7)
+        spread(6)
+        leave_g(5)
+        stats(7)
         norm(4)
+        leave_v(6)
         spread(7)
-        norm(6)
         leave_g(4)
+        centre(7)
         leave_v(7)
-        leave_g(6)

from contextlib import ExitStack

import concourse.mybir as mybir
from concourse.masks import make_identity

FLOPS = 2 * 2 * 1024 * 1024 * 1024

F32 = mybir.dt.float32
BF16 = mybir.dt.bfloat16
U32 = mybir.dt.uint32
U8 = mybir.dt.uint8
E4M3 = mybir.dt.float8_e4m3fn
X4 = mybir.dt.float8_e4m3fn_x4
ACT = mybir.ActivationFunctionType
ALU = mybir.AluOpType

P = 128
D = 1024
NB = 8
EPS = 1e-5
OWN_ON_T = ()
NORM_ON_G = (0, 1)


def tile_efficientfusionlayer_pb_kernel(
    tc, feat, own_self, xbytes, xscale, Wv, bv, Wo, bo, g, be, out
):
    nc = tc.nc
    with ExitStack() as ctx:
        const = ctx.enter_context(tc.tile_pool(name="const", bufs=1))
        ring = ctx.enter_context(tc.tile_pool(name="ring", bufs=1))
        work = ctx.enter_context(tc.tile_pool(name="work", bufs=2))
        psum = ctx.enter_context(tc.psum_pool(name="psum", bufs=1))

        ctx.enter_context(tc.manual_schedule())
        sc = const.tile([P, D], F32, name="sc")
        s_rows = const.tile([P, P], F32, name="s_rows")
        nc.gpsimd.memset(s_rows[:], 0.0)
        nc.scalar.dma_start(out=s_rows[0:8, :], in_=xscale.rearrange("o (c p) -> (o c) p", p=P))
        s_col = const.tile([P, 8], F32, name="s_col")
        wv_raw = [[ring.tile([P, 2, D], BF16, name=f"wv{gg}{tp}", tag="wraw", bufs=10) for tp in range(2)] for gg in range(2)]
        wvsrc = Wv.rearrange("(g m t) k -> g m t k", g=2, t=4)
        xb = [const.tile([P, 2, D], U8, name=f"xb{c}") for c in range(4)]
        xsrc = xbytes.rearrange("(c i p) k -> c p i k", c=4, i=2)

        def load_wv(gg, tp):
            nc.sync.dma_start(out=wv_raw[gg][tp][:], in_=wvsrc[gg, :, 2 * tp : 2 * tp + 2, :])

        def load_x(c):
            nc.sync.dma_start(out=xb[c][:], in_=xsrc[c])

        load_wv(0, 0)
        load_x(0)
        load_wv(0, 1)
        load_x(1)
        load_wv(1, 0)
        load_wv(1, 1)
        load_x(2)
        load_x(3)
        bv_t = const.tile([P, 2, 4], BF16, name="bv_t")
        nc.scalar.dma_start(out=bv_t[:], in_=bv.rearrange("(g p t) -> p g t", g=2, t=4))
        bo_rows = const.tile([P, P], BF16, name="bo_rows")
        nc.gpsimd.memset(bo_rows[:], 0.0)
        nc.scalar.dma_start(out=bo_rows[0:8, :], in_=bo.rearrange("(j p) -> j p", p=P))
        wo_raw = [ring.tile([P, 2, D], BF16, name=f"wo{jp}", tag="wraw", bufs=10) for jp in range(4)]
        wosrc = Wo.rearrange("(q j m) e -> q m j e", q=4, j=2)
        for jp in range(4):
            nc.sync.dma_start(out=wo_raw[jp][:], in_=wosrc[jp])
        g_b = const.tile([P, D], BF16, name="g_b")
        be_b = const.tile([P, D], BF16, name="be_b")
        nc.sync.dma_start(out=g_b[:], in_=g.partition_broadcast(P))
        fo = {}

        def load_fo(i):
            fo[i] = ring.tile([P, 2, D], BF16, name=f"fo{i}", tag="wraw", bufs=10)
            nc.sync.dma_start(out=fo[i][:, 0, :], in_=feat[P * i : P * (i + 1), :])
            nc.sync.dma_start(out=fo[i][:, 1, :], in_=own_self[P * i : P * (i + 1), :])
            if i == 1:
                nc.sync.dma_start(out=be_b[:], in_=be.partition_broadcast(P))

        load_fo(0)
        load_fo(1)
        id32 = const.tile([P, P], F32, name="id32")
        make_identity(nc, id32[:])
        id16 = const.tile([P, P], BF16, name="id16")
        nc.vector.tensor_copy(out=id16[:], in_=id32[:])
        ih16 = const.tile([P, P], BF16, name="ih16")
        nc.vector.tensor_scalar(out=ih16[:], in0=id32[:], scalar1=0.5, scalar2=None, op0=ALU.mult)

        xs = {}
        grouped = {}
        ct = {}

        xc = const.tile([P, 2, D], U32, name="xc", align_bytes=64)
        xsca = const.tile([P, 2, D], U8, name="xsca", align_bytes=64)
        wvc = const.tile([P, 2, D], U32, name="wvc", align_bytes=64)
        wvs = const.tile([P, 2, D], U8, name="wvs", align_bytes=64)
        woc = const.tile([P, 2, D], U32, name="woc", align_bytes=64)
        wos = const.tile([P, 2, D], U8, name="wos", align_bytes=64)
        vg = {}
        vc = const.tile([P, 2, D], U32, name="vc", align_bytes=64)
        vs = const.tile([P, 2, D], U8, name="vs", align_bytes=64)
        boh = const.tile([P, 8], F32, name="boh")

        banks = {}

        def t_turn(kind, n):
            if kind == "x":
                rows = xs[n][:]
            elif kind == "w":
                rows = wv_raw[n // 4][n // 2 % 2][:, n % 2, :]
            else:
                rows = wo_raw[n // 2][:, n % 2, :]
            words = rows.bitcast(F32)
            tag = "g" if kind == "o" else "ps"
            bank = psum.tile([P, 2, 2, P], F32, name="tp", tag=tag, bufs=2 if kind == "o" else 6)
            for h in range(2):
                for u in range(2):
                    nc.tensor.transpose(bank[:, h, u, :], words[:, 256 * h + u : 256 * (h + 1) : 2], id32[:])
            banks[kind, n] = bank

        def e_turn(kind, n):
            if (kind, n // 2) not in grouped:
                grouped[kind, n // 2] = ring.tile(
                    [P, 2, 256, 2], F32, name=f"{kind}{n}", tag="grp", bufs=8, align_bytes=64
                )
            nc.scalar.copy(
                out=grouped[kind, n // 2][:, :, P * (n % 2) : P * (n % 2 + 1), :],
                in_=banks[kind, n][:].rearrange("p h u r -> p h r u"),
            )

        def quant(codes, scales, grouped, cols):
            for h in range(2):
                nc.vector.quantize_mx(
                    out=codes[:, h, cols].bitcast(X4),
                    scales=scales[:, h, cols],
                    in_=grouped[:, h].rearrange("p r u -> p (r u)").bitcast(BF16),
                )

        def scale_x(i):
            xs[i] = ring.tile([P, D], BF16, name=f"xs{i}", tag="xs", bufs=4)
            nc.vector.tensor_tensor(
                out=xs[i][:], in0=xb[i // 2][:, i % 2, :].bitcast(E4M3), in1=sc[:], op=ALU.mult
            )

        s1 = {}

        def stage1(i, gg):
            bank = psum.tile([P, 4, P], F32, name="s1", tag="ps", bufs=6)
            s1[i, gg] = bank
            for t in range(4):
                lc = slice(512 * gg + P * t, 512 * gg + P * (t + 1))
                rc = slice(P * i, P * (i + 1))
                for h in range(2):
                    nc.tensor.matmul_mx(
                        out=bank[:, t, :],
                        lhsT=wvc[:, h, lc].bitcast(X4),
                        lhsT_scale=wvs[:, h, lc],
                        rhs=xc[:, h, rc].bitcast(X4),
                        rhs_scale=xsca[:, h, rc],
                        start=(h == 0),
                        stop=(h == 1),
                    )

        def bias_v(i, gg):
            if (i // 2, gg) not in vg:
                vg[i // 2, gg] = ring.tile([P, 256, 4], BF16, name=f"vg{i}{gg}", tag="vg", bufs=4, align_bytes=64)
            nc.vector.tensor_tensor(
                out=vg[i // 2, gg][:, P * (i % 2) : P * (i % 2 + 1), :],
                in0=s1[i, gg][:].rearrange("p t b -> p b t"),
                in1=bv_t[:, gg, :].unsqueeze(1).to_broadcast([P, P, 4]),
                op=ALU.add,
            )

        n1, vp = {}, {}

        def stage1_pair(q, gg, u):
            bank = psum.tile([P, 2, 256], F32, name="n1", tag="ps", bufs=6)
            n1[q, gg, u] = bank
            rc = slice(256 * q, 256 * (q + 1))
            for a in range(2):
                lc = slice(512 * gg + P * (2 * u + a), 512 * gg + P * (2 * u + a + 1))
                for h in range(2):
                    nc.tensor.matmul_mx(
                        out=bank[:, a, :],
                        lhsT=wvc[:, h, lc].bitcast(X4),
                        lhsT_scale=wvs[:, h, lc],
                        rhs=xc[:, h, rc].bitcast(X4),
                        rhs_scale=xsca[:, h, rc],
                        start=(h == 0),
                        stop=(h == 1),
                    )

        def bias_s(q, gg, u):
            if (q, gg) not in vp:
                vp[q, gg] = ring.tile([P, 4, 256], BF16, name=f"vp{q}{gg}", tag="vp", bufs=2, align_bytes=64)
            for a in range(2):
                t = 2 * u + a
                nc.scalar.activation(
                    out=vp[q, gg][:, t, :], in_=n1[q, gg, u][:, a, :], func=ACT.Identity, bias=bv_t[:, gg, t : t + 1]
                )

        def interleave(q, gg):
            vg[q, gg] = ring.tile([P, 256, 4], BF16, name=f"vg{q}{gg}", tag="vg", bufs=4, align_bytes=64)
            nc.vector.tensor_copy(
                out=vg[q, gg][:].rearrange("p (c i) t -> p c t i", i=4),
                in_=vp[q, gg][:].rearrange("p t (c i) -> p c t i", i=4),
            )

        def quant_v(q):
            for gg in range(2):
                cols = slice(256 * q, 256 * (q + 1))
                nc.vector.quantize_mx(
                    out=vc[:, gg, cols].bitcast(X4),
                    scales=vs[:, gg, cols],
                    in_=vg[q, gg][:].rearrange("p b t -> p (b t)"),
                )

        s2b = {}

        def stage2(q, jj):
            bank = psum.tile([P, 2, 256], F32, name="s2", tag="ps", bufs=6)
            s2b[q, jj] = bank
            ct[q, jj] = ring.tile([P, 2, 256], F32, name=f"ct{q}{jj}", tag="ct", bufs=16)
            rc = slice(256 * q, 256 * (q + 1))
            for a in range(2):
                lc = slice(P * (2 * jj + a), P * (2 * jj + a + 1))
                for gg in range(2):
                    nc.tensor.matmul_mx(
                        out=bank[:, a, :],
                        lhsT=woc[:, gg, lc].bitcast(X4),
                        lhsT_scale=wos[:, gg, lc],
                        rhs=vc[:, gg, rc].bitcast(X4),
                        rhs_scale=vs[:, gg, rc],
                        start=(gg == 0),
                        stop=(gg == 1),
                    )

        def cross_out(q, jj):
            for a in range(2):
                j = 2 * jj + a
                nc.scalar.activation(
                    out=ct[q, jj][:, a, :], in_=s2b[q, jj][:, a, :], func=ACT.Identity, bias=boh[:, j : j + 1], scale=0.5
                )

        zb, zs_, qt, rs, nmean = {}, {}, {}, {}, {}

        def zsum(i):
            sl = slice(P * (i % 2), P * (i % 2 + 1))
            for hd in range(2):
                z = psum.tile([P, 512], F32, name="z", tag="ps", bufs=6)
                cols = slice(512 * hd, 512 * (hd + 1))
                nc.tensor.matmul(out=z[:], lhsT=id16[:], rhs=fo[i][:, 0, cols], start=True, stop=False)
                if i in OWN_ON_T:
                    nc.tensor.matmul(out=z[:], lhsT=ih16[:], rhs=fo[i][:, 1, cols], start=False, stop=False)
                zb[i, hd] = z
            for hd in range(2):
                for jj in range(4):
                    nc.tensor.matmul(
                        out=zb[i, hd][:, P * jj : P * (jj + 1)],
                        lhsT=ct[i // 2, 2 * hd + jj // 2][:, jj % 2, sl],
                        rhs=id32[:],
                        start=False,
                        stop=(jj == 3),
                        is_transpose=True,
                    )

        def stats(i):
            rs[i] = work.tile([P, 1], F32, name="rstd", bufs=8)
            if i in OWN_ON_T:
                st = work.tile([P, 2, 6], F32, name="st", bufs=4)
                mv = work.tile([P, 2], F32, name="mv", bufs=8)
                for hd in range(2):
                    nc.vector.bn_stats(out=st[:, hd, :], in_=zb[i, hd][:])
                nc.vector.bn_aggr(out=mv[:], in_=st[:].rearrange("p a b -> p (a b)"))
                nmean[i] = mv
            else:
                zs = work.tile([P, D], F32, name="zs", bufs=3)
                sm0 = work.tile([P, 1], F32, name="sm0", bufs=8)
                sm1 = work.tile([P, 1], F32, name="sm1", bufs=8)
                nm = work.tile([P, 1], F32, name="nm", bufs=8)
                for hd, sm in ((0, sm0), (1, sm1)):
                    cols = slice(512 * hd, 512 * (hd + 1))
                    nc.vector.scalar_tensor_tensor(
                        out=zs[:, cols], in0=fo[i][:, 1, cols], scalar=0.5, in1=zb[i, hd][:],
                        op0=ALU.mult, op1=ALU.add, accum_out=sm[:],
                    )
                nc.vector.tensor_scalar(
                    out=nm[:], in0=sm0[:], scalar1=sm1[:], scalar2=-1.0 / D, op0=ALU.add, op1=ALU.mult
                )
                zs_[i] = zs
                nmean[i] = nm

        def spread(i):
            if i in OWN_ON_T:
                nc.scalar.activation(out=rs[i][:], in_=nmean[i][:, 1:2], func=ACT.Abs_reciprocal_sqrt, bias=EPS)
                return
            sq = work.tile([P, 1], F32, name="sq", bufs=8)
            junk = work.tile([P, D], BF16, name="junk", bufs=1)
            nc.scalar.activation(out=junk[:], in_=zs_[i][:], func=ACT.Square, bias=nmean[i][:], accum_out=sq[:])
            nc.scalar.activation(out=rs[i][:], in_=sq[:], func=ACT.Abs_reciprocal_sqrt, bias=EPS, scale=1.0 / D)

        def centre(i):
            q = work.tile([P, D], F32, name="q", bufs=4)
            qt[i] = q
            if i in OWN_ON_T:
                for hd in range(2):
                    cols = slice(512 * hd, 512 * (hd + 1))
                    nc.vector.scalar_tensor_tensor(
                        out=q[:, cols], in0=zb[i, hd][:], scalar=nmean[i][:, 0:1], in1=g_b[:, cols],
                        op0=ALU.subtract, op1=ALU.mult,
                    )
            else:
                for hd in range(2):
                    cols = slice(512 * hd, 512 * (hd + 1))
                    nc.vector.scalar_tensor_tensor(
                        out=q[:, cols], in0=zs_[i][:, cols], scalar=nmean[i][:], in1=g_ps[hd][:],
                        op0=ALU.add, op1=ALU.mult,
                    )

        g_ps = []

        def g_bank():
            for hd in range(2):
                bank = psum.tile([P, 512], F32, name="gb", tag="g", bufs=2)
                nc.tensor.matmul(
                    out=bank[:], lhsT=id16[:], rhs=g_b[:, 512 * hd : 512 * (hd + 1)], start=True, stop=True
                )
                g_ps.append(bank)

        def leave_v(i):
            q = qt[i]
            for hd in range(2):
                cols = slice(512 * hd, 512 * (hd + 1))
                nc.vector.scalar_tensor_tensor(
                    out=q[:, cols], in0=q[:, cols], scalar=rs[i][:], in1=be_b[:, cols], op0=ALU.mult, op1=ALU.add
                )
                nc.sync.dma_start(out=out[P * i : P * (i + 1), cols], in_=q[:, cols])

        def norm(i):
            if i in NORM_ON_G:
                qt[i] = work.tile([P, D], F32, name="q", bufs=4)
                shift = work.tile([P, 1], F32, name="shift", bufs=8)
                nc.scalar.activation(out=shift[:], in_=nmean[i][:], func=ACT.Copy, scale=rs[i][:])
                nc.scalar.activation(out=qt[i][:], in_=zs_[i][:], func=ACT.Identity, bias=shift[:], scale=rs[i][:])
                return
            nc.scalar.activation(out=qt[i][:], in_=qt[i][:], func=ACT.Copy, scale=rs[i][:])

        def leave_g(i):
            o = work.tile([P, D], F32, name="o", bufs=3)
            if i in NORM_ON_G:
                nc.gpsimd.tensor_tensor(out=qt[i][:], in0=qt[i][:], in1=g_b[:], op=ALU.mult)
            nc.gpsimd.tensor_tensor(out=o[:], in0=qt[i][:], in1=be_b[:], op=ALU.add)
            nc.sync.dma_start(out=out[P * i : P * (i + 1), :], in_=o[:])

        def cw(gg, tp):
            quant(wvc, wvs, grouped["w", 2 * gg + tp], slice(512 * gg + 256 * tp, 512 * gg + 256 * (tp + 1)))

        def cx(q):
            quant(xc, xsca, grouped["x", q], slice(256 * q, 256 * (q + 1)))

        def cwo(jp):
            quant(woc, wos, grouped["o", jp], slice(256 * jp, 256 * (jp + 1)))

        def cw(n):
            quant(wvc, wvs, grouped["w", n], slice(256 * n, 256 * (n + 1)))

        def cx(q):
            quant(xc, xsca, grouped["x", q], slice(256 * q, 256 * (q + 1)))

        def cwo(jp):
            quant(woc, wos, grouped["o", jp], slice(256 * jp, 256 * (jp + 1)))

        def s_turn():
            banks["s", 0] = psum.tile([P, P], F32, name="st0", tag="ps", bufs=6)
            nc.tensor.transpose(banks["s", 0][:], s_rows[:], id32[:])

        def s_cols():
            nc.scalar.copy(out=s_col[:], in_=banks["s", 0][:, 0:8])

        def s_spread(hd):
            bank = psum.tile([P, 4, P], F32, name="sb", tag="ps", bufs=6)
            for c in range(4):
                nc.tensor.transpose(
                    bank[:, c, :], s_col[:, 4 * hd + c : 4 * hd + c + 1].to_broadcast([P, P]), id32[:]
                )
            banks["sb", hd] = bank

        def s_out(hd):
            copy = nc.vector.tensor_copy if hd else nc.scalar.copy
            copy(out=sc[:, 512 * hd : 512 * (hd + 1)], in_=banks["sb", hd][:].rearrange("p c k -> p (c k)"))

        def bo_t():
            banks["b", 0] = psum.tile([P, P], BF16, name="bot", tag="ps", bufs=6)
            nc.tensor.transpose(banks["b", 0][:], bo_rows[:], id16[:])

        def bo_e():
            nc.scalar.activation(out=boh[:], in_=banks["b", 0][:, 0:8], func=ACT.Copy, scale=0.5)

        s_turn()
        s_cols()
        s_spread(0)
        s_spread(1)
        s_out(0)
        t_turn("w", 1)
        s_out(1)
        t_turn("w", 0)
        e_turn("w", 1)
        scale_x(1)
        t_turn("w", 2)
        e_turn("w", 0)
        t_turn("w", 3)
        scale_x(0)
        t_turn("x", 1)
        e_turn("w", 3)
        t_turn("w", 5)
        e_turn("x", 1)
        scale_x(2)
        t_turn("x", 0)
        e_turn("w", 2)
        t_turn("w", 4)
        e_turn("x", 0)
        scale_x(3)
        t_turn("w", 6)
        e_turn("w", 4)
        t_turn("w", 7)
        load_fo(2)
        load_fo(3)
        load_fo(4)
        load_fo(5)
        e_turn("w", 6)
        e_turn("w", 5)
        cw(1)
        t_turn("o", 0)
        t_turn("x", 3)
        cw(0)
        e_turn("o", 0)
        t_turn("o", 1)
        scale_x(4)
        t_turn("x", 2)
        e_turn("o", 1)
        t_turn("o", 3)
        e_turn("w", 7)
        cx(0)
        t_turn("o", 4)
        e_turn("o", 3)
        t_turn("x", 4)
        e_turn("o", 4)
        cw(3)
        t_turn("o", 7)
        e_turn("x", 2)
        stage1(1, 0)
        cwo(0)
        e_turn("x", 3)
        scale_x(5)
        stage1(0, 0)
        e_turn("o", 7)
        e_turn("x", 4)
        cx(1)
        cw(2)
        bias_v(1, 0)
        t_turn("o", 5)
        bias_v(0, 0)
        bo_t()
        stage1(1, 1)
        bo_e()
        e_turn("o", 5)
        t_turn("o", 6)
        cwo(2)
        stage1(2, 0)
        stage1(0, 1)
        stage1(2, 1)
        scale_x(6)
        bias_v(1, 1)
        bias_v(2, 0)
        t_turn("o", 2)
        load_fo(6)
        load_fo(7)
        bias_v(2, 1)
        t_turn("x", 5)
        bias_v(0, 1)
        stage1(3, 1)
        e_turn("x", 5)
        quant_v(0)
        e_turn("o", 2)
        e_turn("o", 6)
        stage1(3, 0)
        cx(2)
        cwo(1)
        stage2(0, 2)
        stage2(0, 0)
        bias_v(3, 0)
        stage1(5, 0)
        cross_out(0, 2)
        bias_v(3, 1)
        stage2(0, 1)
        cross_out(0, 0)
        cwo(3)
        stage1(4, 0)
        cross_out(0, 1)
        quant_v(1)
        bias_v(5, 0)
        stage1(5, 1)
        stage2(0, 3)
        bias_v(4, 0)
        stage2(1, 3)
        cross_out(0, 3)
        bias_v(5, 1)
        stage1(4, 1)
        scale_x(7)
        stage2(1, 1)
        zsum(0)
        cross_out(1, 1)
        bias_v(4, 1)
        cross_out(1, 3)
        stage2(1, 2)
        stats(0)
        stage2(1, 0)
        cross_out(1, 2)
        g_bank()
        cross_out(1, 0)
        quant_v(2)
        zsum(1)
        spread(0)
        t_turn("x", 7)
        stats(1)
        norm(0)
        zsum(2)
        e_turn("x", 7)
        leave_g(0)
        zsum(3)
        spread(1)
        stats(2)
        t_turn("x", 6)
        norm(1)
        stats(3)
        stage2(2, 3)
        stage2(2, 1)
        e_turn("x", 6)
        stage2(2, 2)
        cross_out(2, 1)
        cx(3)
        stage2(2, 0)
        cross_out(2, 2)
        centre(3)
        leave_g(1)
        stage1(6, 1)
        cross_out(2, 3)
        cross_out(2, 0)
        stage1(6, 0)
        spread(3)
        stage1(7, 0)
        stage1(7, 1)
        bias_v(6, 1)
        bias_v(6, 0)
        zsum(4)
        spread(2)
        bias_v(7, 0)
        bias_v(7, 1)
        centre(2)
        norm(3)
        zsum(5)
        quant_v(3)
        stats(4)
        norm(2)
        leave_g(3)
        stage2(3, 1)
        stage2(3, 0)
        cross_out(3, 1)
        stats(5)
        stage2(3, 3)
        cross_out(3, 0)
        stage2(3, 2)
        cross_out(3, 3)
        leave_g(2)
        cross_out(3, 2)
        centre(5)
        spread(5)
        zsum(6)
        centre(4)
        spread(4)
        zsum(7)
        stats(6)
        norm(5)
        centre(6)
        spread(6)
        leave_g(5)
        stats(7)
        norm(4)
        leave_v(6)
        spread(7)
        leave_g(4)
        centre(7)
        leave_v(7)
